import numpy as np
import ml_dtypes


def mxq(x, axis, fmt="e4m3"):
    dtype, down = {"e4m3": (ml_dtypes.float8_e4m3fn, 7), "e5m2": (ml_dtypes.float8_e5m2, 14)}[fmt]
    v = np.moveaxis(np.asarray(x, np.float32).astype(ml_dtypes.bfloat16).astype(np.float64), axis, -1)
    blocks = v.reshape(v.shape[:-1] + (-1, 32))
    amax = np.abs(blocks).max(-1, keepdims=True)
    byte = np.maximum(np.where(amax > 0, np.frexp(amax)[1] - 1 + 127, 0) - down, 1)
    scale = np.exp2(byte - 127.0)
    codes = (blocks / scale).astype(np.float32).astype(dtype).astype(np.float64)
    return np.moveaxis((codes * scale).reshape(v.shape), -1, axis)


WIDE = False


def mx_kscale(k):
    if not WIDE:
        return np.ones(k)
    levels = np.array([10, -10, 5, -5, 0])
    a = np.random.permutation(np.resize(levels, k // 512 * 4)).reshape(k // 512, 4)
    idx = np.arange(k)
    return np.exp2(a[idx // 512, idx % 128 // 32])


BF16 = ml_dtypes.bfloat16


def bf(x):
    return np.asarray(x, np.float32).astype(BF16)


def f64(x):
    return np.asarray(x).astype(np.float64)


BS, NF, N, J, NOUT = 8, 512, 512, 3, 128
KC = J * NF
EPS = 1e-5


def setup_inputs():
    s = mx_kscale(N)
    c = mx_kscale(NF)
    t = np.tile(c, J)
    nb = N * np.random.choice([0.5, 0.625, 0.75, 0.875], BS)
    wt = np.random.choice([0.25, 0.5, 0.75, 1.0], (BS, 1, N))
    return {"X": bf(np.random.standard_normal((BS, NF, N)) * s[None, None, :] * c[None, :, None]),
            "W": bf(np.random.standard_normal((BS, N, N, J)) / np.sqrt(N) / s[None, None, :, None]),
            "N_batch": bf(nb),
            "mask": bf(wt),
            "cv1_w": bf(np.random.standard_normal((NOUT, KC)) / np.sqrt(KC) / t[None, :]),
            "cv1_b": bf(np.random.standard_normal(NOUT) * 0.5),
            "cv2_w": bf(np.random.standard_normal((NOUT, KC)) / np.sqrt(KC) / t[None, :]),
            "cv2_b": bf(np.random.standard_normal(NOUT) * 0.5),
            "bn_gamma": bf(1.0 + 0.1 * np.random.standard_normal(NOUT + NOUT)),
            "bn_beta": bf(0.3 * np.random.standard_normal(NOUT + NOUT))}


def reference(X, W, N_batch, mask, cv1_w, cv1_b, cv2_w, cv2_b, bn_gamma, bn_beta):
    mk = f64(mask)
    Xq = mxq(f64(X), 2, "e4m3")
    Wq = mxq(f64(W), 2, "e4m3")
    g = Wq.transpose(0, 3, 1, 2) @ Xq.transpose(0, 2, 1)[:, None]
    x1 = g.transpose(0, 1, 3, 2).reshape(BS, KC, N)
    x1q = mxq(x1, 1, "e4m3")
    y1 = (mxq(f64(cv1_w), 1, "e4m3") @ x1q) + f64(cv1_b)[None, :, None]
    z1 = np.maximum(y1, 0.0)
    yl1 = np.maximum((mxq(f64(cv2_w), 1, "e4m3") @ x1q) + f64(cv2_b)[None, :, None], 0.0)
    zb = np.concatenate([yl1, z1], axis=1)
    total = f64(N_batch).sum()
    mean = (zb * mk).sum(axis=(0, 2)) / total
    cz = zb - mean[None, :, None]
    var = (mk * cz * cz).sum(axis=(0, 2)) / total
    zbn = cz * (1.0 / np.sqrt(var + EPS))[None, :, None]
    return (f64(bn_gamma)[None, :, None] * zbn + f64(bn_beta)[None, :, None]) * mk

@@ -1,0 +1,389 @@
+from contextlib import ExitStack
+
+import concourse.mybir as mybir
+from concourse.masks import make_identity
+
+F32 = mybir.dt.float32
+BF16 = mybir.dt.bfloat16
+U32 = mybir.dt.uint32
+U8 = mybir.dt.uint8
+FP8X4 = mybir.dt.float8_e4m3fn_x4
+ALU = mybir.AluOpType
+ACT = mybir.ActivationFunctionType
+AXIS_X = mybir.AxisListType.X
+
+P = 128
+PACK = 4
+GRAPHS = 8
+FEATURES = 512
+NODES = 512
+OPERATORS = 3
+CONVS = 2
+CHANNELS = OPERATORS * FEATURES
+EPS = 1e-5
+
+TILES = 4
+PAIRS = 2
+PAIR_COLS = 2 * P
+WORDS = NODES // 2
+
+FLOPS = 2 * GRAPHS * (OPERATORS * NODES * NODES * FEATURES + CONVS * P * CHANNELS * NODES)
+
+
+def tile_layer_simple_pa_t_kernel(
+    tc, X, W, N_batch, mask, cv1_w, cv1_b, cv2_w, cv2_b, bn_gamma, bn_beta, out
+):
+    nc = tc.nc
+    with ExitStack() as pools:
+        const = pools.enter_context(tc.tile_pool(name="const", bufs=1))
+        w_raw_pool = pools.enter_context(tc.tile_pool(name="w_raw", bufs=2 * PAIRS))
+        w_sorted_pool = pools.enter_context(tc.tile_pool(name="w_sorted", bufs=2 * PAIRS))
+        x_raw_pool = pools.enter_context(tc.tile_pool(name="x_raw", bufs=2))
+        grouped_pool = pools.enter_context(tc.tile_pool(name="grouped", bufs=OPERATORS))
+        operand_pool = pools.enter_context(tc.tile_pool(name="operand", bufs=2))
+        stat_pool = pools.enter_context(tc.tile_pool(name="stat", bufs=4))
+        tr_psum = pools.enter_context(tc.psum_pool(name="tr_psum", bufs=3))
+        x1_psum = pools.enter_context(tc.psum_pool(name="x1_psum", bufs=3))
+        y_psum = pools.enter_context(tc.psum_pool(name="y_psum", bufs=2))
+
+        w_raws, w_sorteds, w_groupeds, w_operands = {}, {}, {}, {}
+        x_raws, x_groupeds, x_operands = {}, {}, {}
+        x1_groupeds, x1_operands = {}, {}
+
+        def live(g):
+            return 0 <= g < GRAPHS
+
+        def load_operators(g, pair):
+            if not live(g):
+                return
+            w_raw = w_raw_pool.tile([P, 2, NODES * OPERATORS], BF16)
+            rows = W[g, PAIR_COLS * pair : PAIR_COLS * (pair + 1)]
+            nc.sync.dma_start(out=w_raw[:], in_=rows.rearrange("(i p) n j -> p i (n j)", p=P))
+            w_raws[g, pair] = w_raw
+
+        def load_features(g):
+            if not live(g):
+                return
+            x_raw = x_raw_pool.tile([P, TILES, NODES], BF16)
+            nc.sync.dma_start(out=x_raw[:], in_=X[g].rearrange("(i p) n -> p i n", p=P))
+            x_raws[g] = x_raw
+
+        load_operators(0, 0)
+        load_features(0)
+        load_operators(0, 1)
+        load_operators(1, 0)
+        load_operators(1, 1)
+        load_features(1)
+
+        cv_raws = []
+        for cv_w in (cv2_w, cv1_w):
+            cv_raw = const.tile([P, CHANNELS], BF16, name="cv_raw%d" % len(cv_raws))
+            nc.sync.dma_start(out=cv_raw[:], in_=cv_w)
+            cv_raws.append(cv_raw)
+
+        mask_all = const.tile([P, GRAPHS, NODES], BF16)
+        nc.sync.dma_start(
+            out=mask_all[:].rearrange("p g m -> p (g m)"),
+            in_=mask.rearrange("g o m -> (g o m)").partition_broadcast(P),
+        )
+
+        ident_f32 = const.tile([P, P], F32)
+        make_identity(nc, ident_f32[:])
+        ident_bf16 = const.tile([P, P], BF16)
+        make_identity(nc, ident_bf16[:])
+        ones_f32 = const.tile([P, P], F32)
+        nc.vector.memset(ones_f32[:], 1.0)
+        eps = const.tile([P, 1], F32)
+        nc.vector.memset(eps[:], EPS)
+
+        warm = const.tile([P, 1], F32)
+        nc.scalar.activation(out=warm[:], in_=eps[:], func=ACT.Sqrt)
+
+        vector_rows = const.tile([P, P], BF16)
+        nc.vector.memset(vector_rows[:], 0.0)
+        nc.scalar.dma_start(out=vector_rows[0:1, :], in_=cv2_b.unsqueeze(0))
+        nc.scalar.dma_start(out=vector_rows[1:2, :], in_=cv1_b.unsqueeze(0))
+        nc.scalar.dma_start(out=vector_rows[2:4, :], in_=bn_gamma.rearrange("(h c) -> h c", h=CONVS))
+        nc.scalar.dma_start(out=vector_rows[4:6, :], in_=bn_beta.rearrange("(h c) -> h c", h=CONVS))
+        vector_cols = tr_psum.tile([P, P], BF16, tag="tr")
+        nc.tensor.transpose(vector_cols[:], vector_rows[:], ident_bf16[:])
+        per_channel = const.tile([P, 3 * CONVS], F32)
+        nc.vector.tensor_copy(out=per_channel[:], in_=vector_cols[:, 0 : 3 * CONVS])
+        bias = per_channel[:, 0:CONVS]
+        gamma = per_channel[:, CONVS : 2 * CONVS]
+        beta = per_channel[:, 2 * CONVS : 3 * CONVS]
+
+        mask_part = const.tile([P, GRAPHS * NODES // P], BF16)
+        nc.scalar.dma_start(
+            out=mask_part[:], in_=mask.rearrange("g o (q r) -> (g o q) r", r=GRAPHS * NODES // P)
+        )
+        counts_row = const.tile([P, GRAPHS], BF16)
+        nc.vector.memset(counts_row[:], 0.0)
+        nc.scalar.dma_start(out=counts_row[0:1, :], in_=N_batch.unsqueeze(0))
+        partial = const.tile([P, 2], F32)
+        nc.vector.reduce_sum(out=partial[:, 0:1], in_=mask_part[:], axis=AXIS_X)
+        nc.vector.reduce_sum(out=partial[:, 1:2], in_=counts_row[:], axis=AXIS_X)
+        totals_psum = tr_psum.tile([P, 2], F32, tag="tr")
+        nc.tensor.matmul(out=totals_psum[:], lhsT=ones_f32[:], rhs=partial[:], start=True, stop=True)
+        totals = const.tile([P, 2], F32)
+        nc.vector.tensor_copy(out=totals[:], in_=totals_psum[:])
+        mask_sum = totals[:, 0:1]
+
+        pivot = const.tile([P, CONVS], F32)
+        nc.vector.tensor_scalar_max(out=pivot[:], in0=bias, scalar1=0.0)
+        inv_total = const.tile([P, 1], F32)
+        nc.vector.reciprocal(out=inv_total[:], in_=totals[:, 1:2])
+        ratio_less_1 = const.tile([P, 1], F32)
+        nc.vector.tensor_scalar(
+            out=ratio_less_1[:], in0=mask_sum, scalar1=inv_total[:], scalar2=-1.0, op0=ALU.mult, op1=ALU.add
+        )
+        ratio_less_2 = const.tile([P, 1], F32)
+        nc.vector.tensor_scalar_add(out=ratio_less_2[:], in0=ratio_less_1[:], scalar1=-1.0)
+        offset_0 = const.tile([P, CONVS], F32)
+        nc.vector.tensor_scalar_mul(out=offset_0[:], in0=pivot[:], scalar1=ratio_less_1[:])
+        twice_offset_0 = const.tile([P, CONVS], F32)
+        nc.vector.tensor_scalar_mul(out=twice_offset_0[:], in0=offset_0[:], scalar1=2.0)
+
+        z = const.tile([P, CONVS, GRAPHS, NODES], F32)
+        first_parts = const.tile([P, CONVS, GRAPHS], F32)
+        second_parts = const.tile([P, CONVS, GRAPHS], F32)
+
+        cv_grouped = const.tile([P, CONVS, OPERATORS, P, PACK], BF16, align_bytes=64)
+        cv_codes = const.tile([P, CONVS, OPERATORS, P], U32, align_bytes=64)
+        cv_scales = const.tile([P, CONVS, OPERATORS, P], U8, align_bytes=64)
+
+        def prepare_conv_weights():
+            for conv in range(CONVS):
+                for j in range(OPERATORS):
+                    cv_t = tr_psum.tile([P, PACK, P], BF16, tag="tr")
+                    for t in range(PACK):
+                        first_channel = FEATURES * j + P * t
+                        nc.tensor.transpose(
+                            cv_t[:, t, :], cv_raws[conv][:, first_channel : first_channel + P], ident_bf16[:]
+                        )
+                    nc.scalar.copy(out=cv_grouped[:, conv, j], in_=cv_t[:].rearrange("p t o -> p o t"))
+            for conv in range(CONVS):
+                for j in range(OPERATORS):
+                    nc.vector.quantize_mx(
+                        out=cv_codes[:, conv, j, :].bitcast(FP8X4),
+                        scales=cv_scales[:, conv, j, :],
+                        in_=cv_grouped[:, conv, j].rearrange("p o t -> p (o t)"),
+                    )
+
+        def transpose_words(bank, rows_of):
+            for u in range(2):
+                for i in range(2):
+                    nc.tensor.transpose(
+                        bank[:, u, P * i : P * (i + 1)],
+                        rows_of(i).bitcast(F32)[:, P * u : P * (u + 1)],
+                        ident_f32[:],
+                    )
+
+        def sort_operators(g, pair):
+            if not live(g):
+                return
+            w_sorted = w_sorted_pool.tile([P, 2, OPERATORS, NODES], BF16)
+            nc.vector.tensor_copy(
+                out=w_sorted[:], in_=w_raws[g, pair][:].rearrange("p i (n j) -> p i j n", j=OPERATORS)
+            )
+            w_sorteds[g, pair] = w_sorted
+
+        def transpose_features(g):
+            if not live(g):
+                return
+            x_grouped = operand_pool.tile([P, FEATURES, PACK], BF16, align_bytes=64)
+            x_groupeds[g] = x_grouped
+            for pair in range(PAIRS):
+                x_t = tr_psum.tile([P, 2, PAIR_COLS], F32, tag="tr")
+                transpose_words(x_t, lambda i: x_raws[g][:, 2 * pair + i, :])
+                copy = nc.vector.tensor_copy if pair == 0 else nc.scalar.copy
+                copy(
+                    out=x_grouped[:].bitcast(F32)[:, PAIR_COLS * pair : PAIR_COLS * (pair + 1), :],
+                    in_=x_t[:].rearrange("p u c -> p c u"),
+                )
+
+        def quantise_features(g):
+            if not live(g):
+                return
+            x_codes = operand_pool.tile([P, FEATURES], U32, align_bytes=64)
+            x_scales = operand_pool.tile([P, FEATURES], U8, align_bytes=64)
+            nc.vector.quantize_mx(
+                out=x_codes[:].bitcast(FP8X4),
+                scales=x_scales[:],
+                in_=x_groupeds[g][:].rearrange("p c t -> p (c t)"),
+            )
+            x_operands[g] = (x_codes, x_scales)
+
+        def transpose_operators(g, pair):
+            if not live(g):
+                return
+            for j in range(OPERATORS):
+                if pair == 0:
+                    w_grouped = grouped_pool.tile([P, NODES, PACK], BF16, align_bytes=64)
+                    w_groupeds[g, j] = w_grouped
+                w_t = tr_psum.tile([P, 2, PAIR_COLS], F32, tag="tr")
+                transpose_words(w_t, lambda i: w_sorteds[g, pair][:, i, j, :])
+                nc.scalar.copy(
+                    out=w_groupeds[g, j][:].bitcast(F32)[:, PAIR_COLS * pair : PAIR_COLS * (pair + 1), :],
+                    in_=w_t[:].rearrange("p u c -> p c u"),
+                )
+
+        def quantise_operators(g):
+            if not live(g):
+                return
+            w_codes = operand_pool.tile([P, OPERATORS, NODES], U32, align_bytes=64)
+            w_scales = operand_pool.tile([P, OPERATORS, NODES], U8, align_bytes=64)
+            for j in range(OPERATORS):
+                nc.vector.quantize_mx(
+                    out=w_codes[:, j, :].bitcast(FP8X4),
+                    scales=w_scales[:, j, :],
+                    in_=w_groupeds[g, j][:].rearrange("p c t -> p (c t)"),
+                )
+            w_operands[g] = (w_codes, w_scales)
+
+        def apply_operator(g, j):
+            if not live(g):
+                return
+            x_codes, x_scales = x_operands[g]
+            w_codes, w_scales = w_operands[g]
+            x1_grouped = grouped_pool.tile([P, NODES, PACK], BF16, align_bytes=64)
+            x1_groupeds[g, j] = x1_grouped
+            for i in range(TILES):
+                m_cols = slice(P * i, P * (i + 1))
+                x1_bank = x1_psum.tile([P, PACK, P], F32)
+                for t in range(PACK):
+                    f_cols = slice(P * t, P * (t + 1))
+                    nc.tensor.matmul_mx(
+                        out=x1_bank[:, t, :],
+                        lhsT=x_codes[:, f_cols].bitcast(FP8X4),
+                        lhsT_scale=x_scales[:, f_cols],
+                        rhs=w_codes[:, j, m_cols].bitcast(FP8X4),
+                        rhs_scale=w_scales[:, j, m_cols],
+                        start=True,
+                        stop=True,
+                    )
+                nc.scalar.copy(out=x1_grouped[:, m_cols, :], in_=x1_bank[:].rearrange("p t m -> p m t"))
+
+        def quantise_x1(g, j):
+            if not live(g):
+                return
+            if j == 0:
+                x1_codes = operand_pool.tile([P, OPERATORS, NODES], U32, align_bytes=64)
+                x1_scales = operand_pool.tile([P, OPERATORS, NODES], U8, align_bytes=64)
+                x1_operands[g] = (x1_codes, x1_scales)
+            x1_codes, x1_scales = x1_operands[g]
+            nc.vector.quantize_mx(
+                out=x1_codes[:, j, :].bitcast(FP8X4),
+                scales=x1_scales[:, j, :],
+                in_=x1_groupeds[g, j][:].rearrange("p m t -> p (m t)"),
+            )
+
+        def convolve(g):
+            if not live(g):
+                return
+            x1_codes, x1_scales = x1_operands[g]
+            for conv in range(CONVS):
+                y = y_psum.tile([P, NODES], F32)
+                for j in range(OPERATORS):
+                    nc.tensor.matmul_mx(
+                        out=y[:],
+                        lhsT=cv_codes[:, conv, j, :].bitcast(FP8X4),
+                        lhsT_scale=cv_scales[:, conv, j, :],
+                        rhs=x1_codes[:, j, :].bitcast(FP8X4),
+                        rhs_scale=x1_scales[:, j, :],
+                        start=(j == 0),
+                        stop=(j == OPERATORS - 1),
+                    )
+                nc.scalar.activation(
+                    out=z[:, conv, g, :], in_=y[:], func=ACT.Relu, bias=bias[:, conv : conv + 1]
+                )
+
+        def add_to_statistics(g):
+            if not live(g):
+                return
+            weighted = []
+            for conv in range(CONVS):
+                masked = stat_pool.tile([P, NODES], F32)
+                nc.vector.scalar_tensor_tensor(
+                    out=masked[:],
+                    in0=z[:, conv, g, :],
+                    scalar=pivot[:, conv : conv + 1],
+                    in1=mask_all[:, g, :],
+                    op0=ALU.subtract,
+                    op1=ALU.mult,
+                    accum_out=first_parts[:, conv, g : g + 1],
+                )
+                weighted.append(masked)
+            for conv in range(CONVS):
+                squares = stat_pool.tile([P, NODES], F32)
+                nc.vector.scalar_tensor_tensor(
+                    out=squares[:],
+                    in0=z[:, conv, g, :],
+                    scalar=pivot[:, conv : conv + 1],
+                    in1=weighted[conv][:],
+                    op0=ALU.subtract,
+                    op1=ALU.mult,
+                    accum_out=second_parts[:, conv, g : g + 1],
+                )
+
+        for step in range(-1, GRAPHS + 2):
+            convolve(step - 2)
+            transpose_features(step)
+            load_features(step + 2)
+            add_to_statistics(step - 2)
+            quantise_features(step)
+            for pair in range(PAIRS):
+                transpose_operators(step, pair)
+            quantise_operators(step)
+            if step == 0:
+                prepare_conv_weights()
+            for j in range(OPERATORS):
+                apply_operator(step - 1, j)
+                quantise_x1(step - 1, j)
+                if j < PAIRS:
+                    sort_operators(step + 1, j)
+                    load_operators(step + 3, j)
+
+        first = const.tile([P, CONVS], F32)
+        nc.vector.reduce_sum(out=first[:], in_=first_parts[:], axis=AXIS_X)
+        second = const.tile([P, CONVS], F32)
+        nc.vector.reduce_sum(out=second[:], in_=second_parts[:], axis=AXIS_X)
+        offset = const.tile([P, CONVS], F32)
+        nc.vector.scalar_tensor_tensor(
+            out=offset[:], in0=first[:], scalar=inv_total[:], in1=offset_0[:], op0=ALU.mult, op1=ALU.add
+        )
+        inner = const.tile([P, CONVS], F32)
+        nc.vector.scalar_tensor_tensor(
+            out=inner[:], in0=offset[:], scalar=ratio_less_2[:], in1=twice_offset_0[:], op0=ALU.mult, op1=ALU.add
+        )
+        correction = const.tile([P, CONVS], F32)
+        nc.vector.tensor_mul(out=correction[:], in0=inner[:], in1=offset[:])
+        var = const.tile([P, CONVS], F32)
+        nc.vector.scalar_tensor_tensor(
+            out=var[:], in0=second[:], scalar=inv_total[:], in1=correction[:], op0=ALU.mult, op1=ALU.add
+        )
+        std = const.tile([P, CONVS], F32)
+        nc.scalar.activation(out=std[:], in_=var[:], func=ACT.Sqrt, bias=eps[:])
+        mean = const.tile([P, CONVS], F32)
+        nc.vector.tensor_add(out=mean[:], in0=offset[:], in1=pivot[:])
+        inv_std = const.tile([P, CONVS], F32)
+        nc.vector.reciprocal(out=inv_std[:], in_=std[:])
+        gain = const.tile([P, CONVS], F32)
+        nc.vector.tensor_mul(out=gain[:], in0=gamma, in1=inv_std[:])
+        mean_gain = const.tile([P, CONVS], F32)
+        nc.vector.tensor_mul(out=mean_gain[:], in0=mean[:], in1=gain[:])
+        shift = const.tile([P, CONVS], F32)
+        nc.vector.tensor_sub(out=shift[:], in0=beta, in1=mean_gain[:])
+
+        for g in range(GRAPHS):
+            for conv in range(CONVS):
+                piece = z[:, conv, g, :]
+                nc.scalar.activation(
+                    out=piece,
+                    in_=piece,
+                    func=ACT.Identity,
+                    scale=gain[:, conv : conv + 1],
+                    bias=shift[:, conv : conv + 1],
+                )
+                nc.vector.tensor_mul(out=piece, in0=piece, in1=mask_all[:, g, :])
+                nc.sync.dma_start(out=out[g, P * conv : P * (conv + 1), :], in_=piece)

@@ -35,6 +35,7 @@ def tile_layer_simple_pa_t_kernel(
 ):
     nc = tc.nc
     with ExitStack() as pools:
+        pools.enter_context(tc.manual_schedule())
         const = pools.enter_context(tc.tile_pool(name="const", bufs=1))
         w_raw_pool = pools.enter_context(tc.tile_pool(name="w_raw", bufs=2 * PAIRS))
         w_sorted_pool = pools.enter_context(tc.tile_pool(name="w_sorted", bufs=2 * PAIRS))
@@ -105,10 +106,7 @@ def tile_layer_simple_pa_t_kernel(
         nc.scalar.dma_start(out=vector_rows[1:2, :], in_=cv1_b.unsqueeze(0))
         nc.scalar.dma_start(out=vector_rows[2:4, :], in_=bn_gamma.rearrange("(h c) -> h c", h=CONVS))
         nc.scalar.dma_start(out=vector_rows[4:6, :], in_=bn_beta.rearrange("(h c) -> h c", h=CONVS))
-        vector_cols = tr_psum.tile([P, P], BF16, tag="tr")
-        nc.tensor.transpose(vector_cols[:], vector_rows[:], ident_bf16[:])
         per_channel = const.tile([P, 3 * CONVS], F32)
-        nc.vector.tensor_copy(out=per_channel[:], in_=vector_cols[:, 0 : 3 * CONVS])
         bias = per_channel[:, 0:CONVS]
         gamma = per_channel[:, CONVS : 2 * CONVS]
         beta = per_channel[:, 2 * CONVS : 3 * CONVS]
@@ -120,29 +118,40 @@ def tile_layer_simple_pa_t_kernel(
         counts_row = const.tile([P, GRAPHS], BF16)
         nc.vector.memset(counts_row[:], 0.0)
         nc.scalar.dma_start(out=counts_row[0:1, :], in_=N_batch.unsqueeze(0))
-        partial = const.tile([P, 2], F32)
-        nc.vector.reduce_sum(out=partial[:, 0:1], in_=mask_part[:], axis=AXIS_X)
-        nc.vector.reduce_sum(out=partial[:, 1:2], in_=counts_row[:], axis=AXIS_X)
-        totals_psum = tr_psum.tile([P, 2], F32, tag="tr")
-        nc.tensor.matmul(out=totals_psum[:], lhsT=ones_f32[:], rhs=partial[:], start=True, stop=True)
-        totals = const.tile([P, 2], F32)
-        nc.vector.tensor_copy(out=totals[:], in_=totals_psum[:])
-        mask_sum = totals[:, 0:1]
 
         pivot = const.tile([P, CONVS], F32)
-        nc.vector.tensor_scalar_max(out=pivot[:], in0=bias, scalar1=0.0)
         inv_total = const.tile([P, 1], F32)
-        nc.vector.reciprocal(out=inv_total[:], in_=totals[:, 1:2])
-        ratio_less_1 = const.tile([P, 1], F32)
-        nc.vector.tensor_scalar(
-            out=ratio_less_1[:], in0=mask_sum, scalar1=inv_total[:], scalar2=-1.0, op0=ALU.mult, op1=ALU.add
-        )
         ratio_less_2 = const.tile([P, 1], F32)
-        nc.vector.tensor_scalar_add(out=ratio_less_2[:], in0=ratio_less_1[:], scalar1=-1.0)
         offset_0 = const.tile([P, CONVS], F32)
-        nc.vector.tensor_scalar_mul(out=offset_0[:], in0=pivot[:], scalar1=ratio_less_1[:])
         twice_offset_0 = const.tile([P, CONVS], F32)
-        nc.vector.tensor_scalar_mul(out=twice_offset_0[:], in0=offset_0[:], scalar1=2.0)
+
+        def prepare_channel_vectors():
+            vector_cols = tr_psum.tile([P, P], BF16, tag="tr")
+            nc.tensor.transpose(vector_cols[:], vector_rows[:], ident_bf16[:])
+            nc.vector.tensor_copy(out=per_channel[:], in_=vector_cols[:, 0 : 3 * CONVS])
+            nc.vector.tensor_scalar_max(out=pivot[:], in0=bias, scalar1=0.0)
+
+            partial = const.tile([P, 2], F32)
+            nc.vector.reduce_sum(out=partial[:, 0:1], in_=mask_part[:], axis=AXIS_X)
+            nc.vector.reduce_sum(out=partial[:, 1:2], in_=counts_row[:], axis=AXIS_X)
+            totals_psum = tr_psum.tile([P, 2], F32, tag="tr")
+            nc.tensor.matmul(out=totals_psum[:], lhsT=ones_f32[:], rhs=partial[:], start=True, stop=True)
+            totals = const.tile([P, 2], F32)
+            nc.vector.tensor_copy(out=totals[:], in_=totals_psum[:])
+
+            nc.vector.reciprocal(out=inv_total[:], in_=totals[:, 1:2])
+            ratio_less_1 = const.tile([P, 1], F32)
+            nc.vector.tensor_scalar(
+                out=ratio_less_1[:],
+                in0=totals[:, 0:1],
+                scalar1=inv_total[:],
+                scalar2=-1.0,
+                op0=ALU.mult,
+                op1=ALU.add,
+            )
+            nc.vector.tensor_scalar_add(out=ratio_less_2[:], in0=ratio_less_1[:], scalar1=-1.0)
+            nc.vector.tensor_scalar_mul(out=offset_0[:], in0=pivot[:], scalar1=ratio_less_1[:])
+            nc.vector.tensor_scalar_mul(out=twice_offset_0[:], in0=offset_0[:], scalar1=2.0)
 
         z = const.tile([P, CONVS, GRAPHS, NODES], F32)
         first_parts = const.tile([P, CONVS, GRAPHS], F32)
@@ -187,6 +196,7 @@ def tile_layer_simple_pa_t_kernel(
                 out=w_sorted[:], in_=w_raws[g, pair][:].rearrange("p i (n j) -> p i j n", j=OPERATORS)
             )
             w_sorteds[g, pair] = w_sorted
+            load_operators(g + 2, pair)
 
         def transpose_features(g):
             if not live(g):
@@ -201,6 +211,7 @@ def tile_layer_simple_pa_t_kernel(
                     out=x_grouped[:].bitcast(F32)[:, PAIR_COLS * pair : PAIR_COLS * (pair + 1), :],
                     in_=x_t[:].rearrange("p u c -> p c u"),
                 )
+            load_features(g + 2)
 
         def quantise_features(g):
             if not live(g):
@@ -329,7 +340,6 @@ def tile_layer_simple_pa_t_kernel(
         for step in range(-1, GRAPHS + 2):
             convolve(step - 2)
             transpose_features(step)
-            load_features(step + 2)
             add_to_statistics(step - 2)
             quantise_features(step)
             for pair in range(PAIRS):
@@ -337,12 +347,12 @@ def tile_layer_simple_pa_t_kernel(
             quantise_operators(step)
             if step == 0:
                 prepare_conv_weights()
+                prepare_channel_vectors()
             for j in range(OPERATORS):
                 apply_operator(step - 1, j)
                 quantise_x1(step - 1, j)
                 if j < PAIRS:
                     sort_operators(step + 1, j)
-                    load_operators(step + 3, j)
 
         first = const.tile([P, CONVS], F32)
         nc.vector.reduce_sum(out=first[:], in_=first_parts[:], axis=AXIS_X)

@@ -18,6 +18,7 @@ GRAPHS = 8
 FEATURES = 512
 NODES = 512
 OPERATORS = 3
+UNITS = GRAPHS * OPERATORS
 CONVS = 2
 CHANNELS = OPERATORS * FEATURES
 EPS = 1e-5
@@ -25,7 +26,13 @@ EPS = 1e-5
 TILES = 4
 PAIRS = 2
 PAIR_COLS = 2 * P
-WORDS = NODES // 2
+
+SORT_AHEAD = 1
+QUANTISE_W_LAG = 1
+STEP_1_LAG = 2
+QUANTISE_X1_LAG = 3
+STEP_2_LAG = 4
+STATISTICS_LAG = 5
 
 FLOPS = 2 * GRAPHS * (OPERATORS * NODES * NODES * FEATURES + CONVS * P * CHANNELS * NODES)
 
@@ -35,52 +42,44 @@ def tile_layer_simple_pa_t_kernel(
 ):
     nc = tc.nc
     with ExitStack() as pools:
-        pools.enter_context(tc.manual_schedule())
         const = pools.enter_context(tc.tile_pool(name="const", bufs=1))
-        w_raw_pool = pools.enter_context(tc.tile_pool(name="w_raw", bufs=2 * PAIRS))
-        w_sorted_pool = pools.enter_context(tc.tile_pool(name="w_sorted", bufs=2 * PAIRS))
-        x_raw_pool = pools.enter_context(tc.tile_pool(name="x_raw", bufs=2))
-        grouped_pool = pools.enter_context(tc.tile_pool(name="grouped", bufs=OPERATORS))
-        operand_pool = pools.enter_context(tc.tile_pool(name="operand", bufs=2))
+        raw_pool = pools.enter_context(tc.tile_pool(name="raw", bufs=2))
+        unit_pool = pools.enter_context(tc.tile_pool(name="unit", bufs=3))
+        graph_pool = pools.enter_context(tc.tile_pool(name="graph", bufs=2))
         stat_pool = pools.enter_context(tc.tile_pool(name="stat", bufs=4))
         tr_psum = pools.enter_context(tc.psum_pool(name="tr_psum", bufs=3))
         x1_psum = pools.enter_context(tc.psum_pool(name="x1_psum", bufs=3))
-        y_psum = pools.enter_context(tc.psum_pool(name="y_psum", bufs=2))
+        y_psum = pools.enter_context(tc.psum_pool(name="y_psum", bufs=CONVS))
 
-        w_raws, w_sorteds, w_groupeds, w_operands = {}, {}, {}, {}
-        x_raws, x_groupeds, x_operands = {}, {}, {}
-        x1_groupeds, x1_operands = {}, {}
+        w_raws, x_raws, x_groupeds, x_operands, y_banks = {}, {}, {}, {}, {}
+        w_sorteds, w_groupeds, w_operands, x1_groupeds, x1_operands = {}, {}, {}, {}, {}
 
-        def live(g):
-            return 0 <= g < GRAPHS
+        def live(unit):
+            return 0 <= unit < UNITS
 
-        def load_operators(g, pair):
-            if not live(g):
+        def load_operators(g):
+            if g >= GRAPHS:
                 return
-            w_raw = w_raw_pool.tile([P, 2, NODES * OPERATORS], BF16)
-            rows = W[g, PAIR_COLS * pair : PAIR_COLS * (pair + 1)]
-            nc.sync.dma_start(out=w_raw[:], in_=rows.rearrange("(i p) n j -> p i (n j)", p=P))
-            w_raws[g, pair] = w_raw
+            w_raw = raw_pool.tile([P, TILES, NODES * OPERATORS], BF16)
+            nc.sync.dma_start(out=w_raw[:], in_=W[g].rearrange("(i p) n j -> p i (n j)", p=P))
+            w_raws[g] = w_raw
 
         def load_features(g):
-            if not live(g):
+            if g >= GRAPHS:
                 return
-            x_raw = x_raw_pool.tile([P, TILES, NODES], BF16)
+            x_raw = raw_pool.tile([P, TILES, NODES], BF16)
             nc.sync.dma_start(out=x_raw[:], in_=X[g].rearrange("(i p) n -> p i n", p=P))
             x_raws[g] = x_raw
 
-        load_operators(0, 0)
+        load_operators(0)
         load_features(0)
-        load_operators(0, 1)
-        load_operators(1, 0)
-        load_operators(1, 1)
-        load_features(1)
-
         cv_raws = []
         for cv_w in (cv2_w, cv1_w):
             cv_raw = const.tile([P, CHANNELS], BF16, name="cv_raw%d" % len(cv_raws))
             nc.sync.dma_start(out=cv_raw[:], in_=cv_w)
             cv_raws.append(cv_raw)
+        load_operators(1)
+        load_features(1)
 
         mask_all = const.tile([P, GRAPHS, NODES], BF16)
         nc.sync.dma_start(
@@ -161,7 +160,7 @@ def tile_layer_simple_pa_t_kernel(
         cv_codes = const.tile([P, CONVS, OPERATORS, P], U32, align_bytes=64)
         cv_scales = const.tile([P, CONVS, OPERATORS, P], U8, align_bytes=64)
 
-        def prepare_conv_weights():
+        def transpose_conv_weights():
             for conv in range(CONVS):
                 for j in range(OPERATORS):
                     cv_t = tr_psum.tile([P, PACK, P], BF16, tag="tr")
@@ -171,6 +170,8 @@ def tile_layer_simple_pa_t_kernel(
                             cv_t[:, t, :], cv_raws[conv][:, first_channel : first_channel + P], ident_bf16[:]
                         )
                     nc.scalar.copy(out=cv_grouped[:, conv, j], in_=cv_t[:].rearrange("p t o -> p o t"))
+
+        def quantise_conv_weights():
             for conv in range(CONVS):
                 for j in range(OPERATORS):
                     nc.vector.quantize_mx(
@@ -188,77 +189,69 @@ def tile_layer_simple_pa_t_kernel(
                         ident_f32[:],
                     )
 
-        def sort_operators(g, pair):
-            if not live(g):
+        def sort_operator(unit):
+            if not live(unit):
                 return
-            w_sorted = w_sorted_pool.tile([P, 2, OPERATORS, NODES], BF16)
+            g, j = divmod(unit, OPERATORS)
+            w_sorted = unit_pool.tile([P, TILES, NODES], BF16)
             nc.vector.tensor_copy(
-                out=w_sorted[:], in_=w_raws[g, pair][:].rearrange("p i (n j) -> p i j n", j=OPERATORS)
+                out=w_sorted[:], in_=w_raws[g][:].rearrange("p i (n j) -> p i n j", j=OPERATORS)[:, :, :, j]
             )
-            w_sorteds[g, pair] = w_sorted
-            load_operators(g + 2, pair)
+            w_sorteds[unit] = w_sorted
+            if j == OPERATORS - 1:
+                load_operators(g + 2)
 
-        def transpose_features(g):
-            if not live(g):
+        def transpose_features(unit):
+            g, j = divmod(unit, OPERATORS)
+            if not live(unit) or j != 0:
                 return
-            x_grouped = operand_pool.tile([P, FEATURES, PACK], BF16, align_bytes=64)
+            x_grouped = graph_pool.tile([P, FEATURES, PACK], BF16, align_bytes=64)
             x_groupeds[g] = x_grouped
             for pair in range(PAIRS):
                 x_t = tr_psum.tile([P, 2, PAIR_COLS], F32, tag="tr")
                 transpose_words(x_t, lambda i: x_raws[g][:, 2 * pair + i, :])
-                copy = nc.vector.tensor_copy if pair == 0 else nc.scalar.copy
-                copy(
+                nc.vector.tensor_copy(
                     out=x_grouped[:].bitcast(F32)[:, PAIR_COLS * pair : PAIR_COLS * (pair + 1), :],
                     in_=x_t[:].rearrange("p u c -> p c u"),
                 )
             load_features(g + 2)
 
-        def quantise_features(g):
-            if not live(g):
+        def transpose_operator(unit):
+            if not live(unit):
                 return
-            x_codes = operand_pool.tile([P, FEATURES], U32, align_bytes=64)
-            x_scales = operand_pool.tile([P, FEATURES], U8, align_bytes=64)
-            nc.vector.quantize_mx(
-                out=x_codes[:].bitcast(FP8X4),
-                scales=x_scales[:],
-                in_=x_groupeds[g][:].rearrange("p c t -> p (c t)"),
-            )
-            x_operands[g] = (x_codes, x_scales)
-
-        def transpose_operators(g, pair):
-            if not live(g):
-                return
-            for j in range(OPERATORS):
-                if pair == 0:
-                    w_grouped = grouped_pool.tile([P, NODES, PACK], BF16, align_bytes=64)
-                    w_groupeds[g, j] = w_grouped
+            w_grouped = unit_pool.tile([P, NODES, PACK], BF16, align_bytes=64)
+            w_groupeds[unit] = w_grouped
+            for pair in range(PAIRS):
                 w_t = tr_psum.tile([P, 2, PAIR_COLS], F32, tag="tr")
-                transpose_words(w_t, lambda i: w_sorteds[g, pair][:, i, j, :])
+                transpose_words(w_t, lambda i: w_sorteds[unit][:, 2 * pair + i, :])
                 nc.scalar.copy(
-                    out=w_groupeds[g, j][:].bitcast(F32)[:, PAIR_COLS * pair : PAIR_COLS * (pair + 1), :],
+                    out=w_grouped[:].bitcast(F32)[:, PAIR_COLS * pair : PAIR_COLS * (pair + 1), :],
                     in_=w_t[:].rearrange("p u c -> p c u"),
                 )
 
-        def quantise_operators(g):
-            if not live(g):
-                return
-            w_codes = operand_pool.tile([P, OPERATORS, NODES], U32, align_bytes=64)
-            w_scales = operand_pool.tile([P, OPERATORS, NODES], U8, align_bytes=64)
-            for j in range(OPERATORS):
-                nc.vector.quantize_mx(
-                    out=w_codes[:, j, :].bitcast(FP8X4),
-                    scales=w_scales[:, j, :],
-                    in_=w_groupeds[g, j][:].rearrange("p c t -> p (c t)"),
-                )
-            w_operands[g] = (w_codes, w_scales)
+        def quantise(grouped, pool, kind):
+            codes = pool.tile([P, NODES], U32, align_bytes=64, name=kind + "_codes")
+            scales = pool.tile([P, NODES], U8, align_bytes=64, name=kind + "_scales")
+            nc.vector.quantize_mx(
+                out=codes[:].bitcast(FP8X4), scales=scales[:], in_=grouped[:].rearrange("p c t -> p (c t)")
+            )
+            return codes, scales
 
-        def apply_operator(g, j):
-            if not live(g):
+        def quantise_operator(unit):
+            if not live(unit):
                 return
-            x_codes, x_scales = x_operands[g]
-            w_codes, w_scales = w_operands[g]
-            x1_grouped = grouped_pool.tile([P, NODES, PACK], BF16, align_bytes=64)
-            x1_groupeds[g, j] = x1_grouped
+            g, j = divmod(unit, OPERATORS)
+            w_operands[unit] = quantise(w_groupeds[unit], unit_pool, "w")
+            if j == 0:
+                x_operands[g] = quantise(x_groupeds[g], graph_pool, "x")
+
+        def apply_operator(unit):
+            if not live(unit):
+                return
+            x_codes, x_scales = x_operands[unit // OPERATORS]
+            w_codes, w_scales = w_operands[unit]
+            x1_grouped = unit_pool.tile([P, NODES, PACK], BF16, align_bytes=64)
+            x1_groupeds[unit] = x1_grouped
             for i in range(TILES):
                 m_cols = slice(P * i, P * (i + 1))
                 x1_bank = x1_psum.tile([P, PACK, P], F32)
@@ -268,49 +261,47 @@ def tile_layer_simple_pa_t_kernel(
                         out=x1_bank[:, t, :],
                         lhsT=x_codes[:, f_cols].bitcast(FP8X4),
                         lhsT_scale=x_scales[:, f_cols],
-                        rhs=w_codes[:, j, m_cols].bitcast(FP8X4),
-                        rhs_scale=w_scales[:, j, m_cols],
+                        rhs=w_codes[:, m_cols].bitcast(FP8X4),
+                        rhs_scale=w_scales[:, m_cols],
                         start=True,
                         stop=True,
                     )
                 nc.scalar.copy(out=x1_grouped[:, m_cols, :], in_=x1_bank[:].rearrange("p t m -> p m t"))
 
-        def quantise_x1(g, j):
-            if not live(g):
-                return
-            if j == 0:
-                x1_codes = operand_pool.tile([P, OPERATORS, NODES], U32, align_bytes=64)
-                x1_scales = operand_pool.tile([P, OPERATORS, NODES], U8, align_bytes=64)
-                x1_operands[g] = (x1_codes, x1_scales)
-            x1_codes, x1_scales = x1_operands[g]
-            nc.vector.quantize_mx(
-                out=x1_codes[:, j, :].bitcast(FP8X4),
-                scales=x1_scales[:, j, :],
-                in_=x1_groupeds[g, j][:].rearrange("p m t -> p (m t)"),
-            )
+        def quantise_x1(unit):
+            if live(unit):
+                x1_operands[unit] = quantise(x1_groupeds[unit], unit_pool, "x1")
 
-        def convolve(g):
-            if not live(g):
+        def convolve(unit):
+            if not live(unit):
                 return
-            x1_codes, x1_scales = x1_operands[g]
+            g, j = divmod(unit, OPERATORS)
+            x1_codes, x1_scales = x1_operands[unit]
             for conv in range(CONVS):
-                y = y_psum.tile([P, NODES], F32)
-                for j in range(OPERATORS):
-                    nc.tensor.matmul_mx(
-                        out=y[:],
-                        lhsT=cv_codes[:, conv, j, :].bitcast(FP8X4),
-                        lhsT_scale=cv_scales[:, conv, j, :],
-                        rhs=x1_codes[:, j, :].bitcast(FP8X4),
-                        rhs_scale=x1_scales[:, j, :],
-                        start=(j == 0),
-                        stop=(j == OPERATORS - 1),
-                    )
-                nc.scalar.activation(
-                    out=z[:, conv, g, :], in_=y[:], func=ACT.Relu, bias=bias[:, conv : conv + 1]
+                if j == 0:
+                    y = y_psum.tile([P, NODES], F32)
+                    y_banks[g, conv] = y
+                nc.tensor.matmul_mx(
+                    out=y_banks[g, conv][:],
+                    lhsT=cv_codes[:, conv, j, :].bitcast(FP8X4),
+                    lhsT_scale=cv_scales[:, conv, j, :],
+                    rhs=x1_codes[:].bitcast(FP8X4),
+                    rhs_scale=x1_scales[:],
+                    start=(j == 0),
+                    stop=(j == OPERATORS - 1),
                 )
+            if j == OPERATORS - 1:
+                for conv in range(CONVS):
+                    nc.scalar.activation(
+                        out=z[:, conv, g, :],
+                        in_=y_banks[g, conv][:],
+                        func=ACT.Relu,
+                        bias=bias[:, conv : conv + 1],
+                    )
 
-        def add_to_statistics(g):
-            if not live(g):
+        def add_to_statistics(unit):
+            g, j = divmod(unit, OPERATORS)
+            if not live(unit) or j != OPERATORS - 1:
                 return
             weighted = []
             for conv in range(CONVS):
@@ -337,22 +328,20 @@ def tile_layer_simple_pa_t_kernel(
                     accum_out=second_parts[:, conv, g : g + 1],
                 )
 
-        for step in range(-1, GRAPHS + 2):
-            convolve(step - 2)
-            transpose_features(step)
-            add_to_statistics(step - 2)
-            quantise_features(step)
-            for pair in range(PAIRS):
-                transpose_operators(step, pair)
-            quantise_operators(step)
-            if step == 0:
-                prepare_conv_weights()
+        for turn in range(-SORT_AHEAD, UNITS + STATISTICS_LAG + 1):
+            transpose_features(turn)
+            transpose_operator(turn)
+            if turn == 0:
+                transpose_conv_weights()
+            apply_operator(turn - STEP_1_LAG)
+            convolve(turn - STEP_2_LAG)
+            quantise_x1(turn - QUANTISE_X1_LAG)
+            quantise_operator(turn - QUANTISE_W_LAG)
+            if turn == 1:
+                quantise_conv_weights()
                 prepare_channel_vectors()
-            for j in range(OPERATORS):
-                apply_operator(step - 1, j)
-                quantise_x1(step - 1, j)
-                if j < PAIRS:
-                    sort_operators(step + 1, j)
+            add_to_statistics(turn - STATISTICS_LAG)
+            sort_operator(turn + SORT_AHEAD)
 
         first = const.tile([P, CONVS], F32)
         nc.vector.reduce_sum(out=first[:], in_=first_parts[:], axis=AXIS_X)

@@ -44,7 +44,7 @@ def tile_layer_simple_pa_t_kernel(
     with ExitStack() as pools:
         const = pools.enter_context(tc.tile_pool(name="const", bufs=1))
         raw_pool = pools.enter_context(tc.tile_pool(name="raw", bufs=2))
-        unit_pool = pools.enter_context(tc.tile_pool(name="unit", bufs=3))
+        unit_pool = pools.enter_context(tc.tile_pool(name="unit", bufs=4))
         graph_pool = pools.enter_context(tc.tile_pool(name="graph", bufs=2))
         stat_pool = pools.enter_context(tc.tile_pool(name="stat", bufs=4))
         tr_psum = pools.enter_context(tc.psum_pool(name="tr_psum", bufs=3))
@@ -153,8 +153,9 @@ def tile_layer_simple_pa_t_kernel(
             nc.vector.tensor_scalar_mul(out=twice_offset_0[:], in0=offset_0[:], scalar1=2.0)
 
         z = const.tile([P, CONVS, GRAPHS, NODES], F32)
-        first_parts = const.tile([P, CONVS, GRAPHS], F32)
-        second_parts = const.tile([P, CONVS, GRAPHS], F32)
+        sum_parts = const.tile([P, 2, CONVS, GRAPHS], F32)
+        first_parts = sum_parts[:, 0]
+        second_parts = sum_parts[:, 1]
 
         cv_grouped = const.tile([P, CONVS, OPERATORS, P, PACK], BF16, align_bytes=64)
         cv_codes = const.tile([P, CONVS, OPERATORS, P], U32, align_bytes=64)
@@ -343,36 +344,44 @@ def tile_layer_simple_pa_t_kernel(
             add_to_statistics(turn - STATISTICS_LAG)
             sort_operator(turn + SORT_AHEAD)
 
-        first = const.tile([P, CONVS], F32)
-        nc.vector.reduce_sum(out=first[:], in_=first_parts[:], axis=AXIS_X)
-        second = const.tile([P, CONVS], F32)
-        nc.vector.reduce_sum(out=second[:], in_=second_parts[:], axis=AXIS_X)
+        sums = const.tile([P, 2, CONVS], F32)
+        nc.vector.reduce_sum(out=sums[:], in_=sum_parts[:], axis=AXIS_X)
         offset = const.tile([P, CONVS], F32)
-        nc.vector.scalar_tensor_tensor(
-            out=offset[:], in0=first[:], scalar=inv_total[:], in1=offset_0[:], op0=ALU.mult, op1=ALU.add
-        )
         inner = const.tile([P, CONVS], F32)
-        nc.vector.scalar_tensor_tensor(
-            out=inner[:], in0=offset[:], scalar=ratio_less_2[:], in1=twice_offset_0[:], op0=ALU.mult, op1=ALU.add
-        )
         correction = const.tile([P, CONVS], F32)
-        nc.vector.tensor_mul(out=correction[:], in0=inner[:], in1=offset[:])
         var = const.tile([P, CONVS], F32)
-        nc.vector.scalar_tensor_tensor(
-            out=var[:], in0=second[:], scalar=inv_total[:], in1=correction[:], op0=ALU.mult, op1=ALU.add
-        )
         std = const.tile([P, CONVS], F32)
-        nc.scalar.activation(out=std[:], in_=var[:], func=ACT.Sqrt, bias=eps[:])
-        mean = const.tile([P, CONVS], F32)
-        nc.vector.tensor_add(out=mean[:], in0=offset[:], in1=pivot[:])
+        minus_mean = const.tile([P, CONVS], F32)
         inv_std = const.tile([P, CONVS], F32)
-        nc.vector.reciprocal(out=inv_std[:], in_=std[:])
         gain = const.tile([P, CONVS], F32)
-        nc.vector.tensor_mul(out=gain[:], in0=gamma, in1=inv_std[:])
-        mean_gain = const.tile([P, CONVS], F32)
-        nc.vector.tensor_mul(out=mean_gain[:], in0=mean[:], in1=gain[:])
         shift = const.tile([P, CONVS], F32)
-        nc.vector.tensor_sub(out=shift[:], in0=beta, in1=mean_gain[:])
+        columns = [slice(conv, conv + 1) for conv in range(CONVS)]
+        for c in columns:
+            nc.vector.tensor_scalar(
+                out=offset[:, c], in0=sums[:, 0, c], scalar1=inv_total[:], scalar2=offset_0[:, c], op0=ALU.mult, op1=ALU.add
+            )
+        for c in columns:
+            nc.vector.tensor_scalar(
+                out=inner[:, c], in0=offset[:, c], scalar1=ratio_less_2[:], scalar2=twice_offset_0[:, c], op0=ALU.mult, op1=ALU.add
+            )
+        for c in columns:
+            nc.vector.tensor_mul(out=correction[:, c], in0=inner[:, c], in1=offset[:, c])
+        for c in columns:
+            nc.vector.tensor_scalar(
+                out=var[:, c], in0=sums[:, 1, c], scalar1=inv_total[:], scalar2=correction[:, c], op0=ALU.mult, op1=ALU.add
+            )
+        nc.scalar.activation(out=std[:], in_=var[:], func=ACT.Sqrt, bias=eps[:])
+        for c in columns:
+            nc.vector.tensor_scalar(
+                out=minus_mean[:, c], in0=offset[:, c], scalar1=-1.0, scalar2=pivot[:, c], op0=ALU.mult, op1=ALU.subtract
+            )
+        nc.vector.reciprocal(out=inv_std[:], in_=std[:])
+        for c in columns:
+            nc.vector.tensor_mul(out=gain[:, c], in0=gamma[:, c], in1=inv_std[:, c])
+        for c in columns:
+            nc.vector.tensor_scalar(
+                out=shift[:, c], in0=gain[:, c], scalar1=minus_mean[:, c], scalar2=beta[:, c], op0=ALU.mult, op1=ALU.add
+            )
 
         for g in range(GRAPHS):
             for conv in range(CONVS):

@@ -44,7 +44,7 @@ def tile_layer_simple_pa_t_kernel(
     with ExitStack() as pools:
         const = pools.enter_context(tc.tile_pool(name="const", bufs=1))
         raw_pool = pools.enter_context(tc.tile_pool(name="raw", bufs=2))
-        unit_pool = pools.enter_context(tc.tile_pool(name="unit", bufs=4))
+        unit_pool = pools.enter_context(tc.tile_pool(name="unit", bufs=3))
         graph_pool = pools.enter_context(tc.tile_pool(name="graph", bufs=2))
         stat_pool = pools.enter_context(tc.tile_pool(name="stat", bufs=4))
         tr_psum = pools.enter_context(tc.psum_pool(name="tr_psum", bufs=3))
@@ -153,9 +153,8 @@ def tile_layer_simple_pa_t_kernel(
             nc.vector.tensor_scalar_mul(out=twice_offset_0[:], in0=offset_0[:], scalar1=2.0)
 
         z = const.tile([P, CONVS, GRAPHS, NODES], F32)
-        sum_parts = const.tile([P, 2, CONVS, GRAPHS], F32)
-        first_parts = sum_parts[:, 0]
-        second_parts = sum_parts[:, 1]
+        first_parts = const.tile([P, CONVS, GRAPHS], F32)
+        second_parts = const.tile([P, CONVS, GRAPHS], F32)
 
         cv_grouped = const.tile([P, CONVS, OPERATORS, P, PACK], BF16, align_bytes=64)
         cv_codes = const.tile([P, CONVS, OPERATORS, P], U32, align_bytes=64)
@@ -211,7 +210,8 @@ def tile_layer_simple_pa_t_kernel(
             for pair in range(PAIRS):
                 x_t = tr_psum.tile([P, 2, PAIR_COLS], F32, tag="tr")
                 transpose_words(x_t, lambda i: x_raws[g][:, 2 * pair + i, :])
-                nc.vector.tensor_copy(
+                copy = nc.vector.tensor_copy if pair == 0 else nc.scalar.copy
+                copy(
                     out=x_grouped[:].bitcast(F32)[:, PAIR_COLS * pair : PAIR_COLS * (pair + 1), :],
                     in_=x_t[:].rearrange("p u c -> p c u"),
                 )
@@ -344,44 +344,36 @@ def tile_layer_simple_pa_t_kernel(
             add_to_statistics(turn - STATISTICS_LAG)
             sort_operator(turn + SORT_AHEAD)
 
-        sums = const.tile([P, 2, CONVS], F32)
-        nc.vector.reduce_sum(out=sums[:], in_=sum_parts[:], axis=AXIS_X)
+        first = const.tile([P, CONVS], F32)
+        nc.vector.reduce_sum(out=first[:], in_=first_parts[:], axis=AXIS_X)
+        second = const.tile([P, CONVS], F32)
+        nc.vector.reduce_sum(out=second[:], in_=second_parts[:], axis=AXIS_X)
         offset = const.tile([P, CONVS], F32)
+        nc.vector.scalar_tensor_tensor(
+            out=offset[:], in0=first[:], scalar=inv_total[:], in1=offset_0[:], op0=ALU.mult, op1=ALU.add
+        )
         inner = const.tile([P, CONVS], F32)
+        nc.vector.scalar_tensor_tensor(
+            out=inner[:], in0=offset[:], scalar=ratio_less_2[:], in1=twice_offset_0[:], op0=ALU.mult, op1=ALU.add
+        )
         correction = const.tile([P, CONVS], F32)
+        nc.vector.tensor_mul(out=correction[:], in0=inner[:], in1=offset[:])
         var = const.tile([P, CONVS], F32)
+        nc.vector.scalar_tensor_tensor(
+            out=var[:], in0=second[:], scalar=inv_total[:], in1=correction[:], op0=ALU.mult, op1=ALU.add
+        )
         std = const.tile([P, CONVS], F32)
-        minus_mean = const.tile([P, CONVS], F32)
-        inv_std = const.tile([P, CONVS], F32)
-        gain = const.tile([P, CONVS], F32)
-        shift = const.tile([P, CONVS], F32)
-        columns = [slice(conv, conv + 1) for conv in range(CONVS)]
-        for c in columns:
-            nc.vector.tensor_scalar(
-                out=offset[:, c], in0=sums[:, 0, c], scalar1=inv_total[:], scalar2=offset_0[:, c], op0=ALU.mult, op1=ALU.add
-            )
-        for c in columns:
-            nc.vector.tensor_scalar(
-                out=inner[:, c], in0=offset[:, c], scalar1=ratio_less_2[:], scalar2=twice_offset_0[:, c], op0=ALU.mult, op1=ALU.add
-            )
-        for c in columns:
-            nc.vector.tensor_mul(out=correction[:, c], in0=inner[:, c], in1=offset[:, c])
-        for c in columns:
-            nc.vector.tensor_scalar(
-                out=var[:, c], in0=sums[:, 1, c], scalar1=inv_total[:], scalar2=correction[:, c], op0=ALU.mult, op1=ALU.add
-            )
         nc.scalar.activation(out=std[:], in_=var[:], func=ACT.Sqrt, bias=eps[:])
-        for c in columns:
-            nc.vector.tensor_scalar(
-                out=minus_mean[:, c], in0=offset[:, c], scalar1=-1.0, scalar2=pivot[:, c], op0=ALU.mult, op1=ALU.subtract
-            )
+        mean = const.tile([P, CONVS], F32)
+        nc.vector.tensor_add(out=mean[:], in0=offset[:], in1=pivot[:])
+        inv_std = const.tile([P, CONVS], F32)
         nc.vector.reciprocal(out=inv_std[:], in_=std[:])
-        for c in columns:
-            nc.vector.tensor_mul(out=gain[:, c], in0=gamma[:, c], in1=inv_std[:, c])
-        for c in columns:
-            nc.vector.tensor_scalar(
-                out=shift[:, c], in0=gain[:, c], scalar1=minus_mean[:, c], scalar2=beta[:, c], op0=ALU.mult, op1=ALU.add
-            )
+        gain = const.tile([P, CONVS], F32)
+        nc.vector.tensor_mul(out=gain[:], in0=gamma, in1=inv_std[:])
+        mean_gain = const.tile([P, CONVS], F32)
+        nc.vector.tensor_mul(out=mean_gain[:], in0=mean[:], in1=gain[:])
+        shift = const.tile([P, CONVS], F32)
+        nc.vector.tensor_sub(out=shift[:], in0=beta, in1=mean_gain[:])
 
         for g in range(GRAPHS):
             for conv in range(CONVS):

from contextlib import ExitStack

import concourse.mybir as mybir
from concourse.masks import make_identity

F32 = mybir.dt.float32
BF16 = mybir.dt.bfloat16
U32 = mybir.dt.uint32
U8 = mybir.dt.uint8
FP8X4 = mybir.dt.float8_e4m3fn_x4
ALU = mybir.AluOpType
ACT = mybir.ActivationFunctionType
AXIS_X = mybir.AxisListType.X

P = 128
PACK = 4
GRAPHS = 8
FEATURES = 512
NODES = 512
OPERATORS = 3
UNITS = GRAPHS * OPERATORS
CONVS = 2
CHANNELS = OPERATORS * FEATURES
EPS = 1e-5

TILES = 4
PAIRS = 2
PAIR_COLS = 2 * P

SORT_AHEAD = 1
QUANTISE_W_LAG = 1
STEP_1_LAG = 2
QUANTISE_X1_LAG = 3
STEP_2_LAG = 4
STATISTICS_LAG = 5

FLOPS = 2 * GRAPHS * (OPERATORS * NODES * NODES * FEATURES + CONVS * P * CHANNELS * NODES)


def tile_layer_simple_pa_t_kernel(
    tc, X, W, N_batch, mask, cv1_w, cv1_b, cv2_w, cv2_b, bn_gamma, bn_beta, out
):
    nc = tc.nc
    with ExitStack() as pools:
        const = pools.enter_context(tc.tile_pool(name="const", bufs=1))
        raw_pool = pools.enter_context(tc.tile_pool(name="raw", bufs=2))
        unit_pool = pools.enter_context(tc.tile_pool(name="unit", bufs=3))
        graph_pool = pools.enter_context(tc.tile_pool(name="graph", bufs=2))
        stat_pool = pools.enter_context(tc.tile_pool(name="stat", bufs=4))
        tr_psum = pools.enter_context(tc.psum_pool(name="tr_psum", bufs=3))
        x1_psum = pools.enter_context(tc.psum_pool(name="x1_psum", bufs=3))
        y_psum = pools.enter_context(tc.psum_pool(name="y_psum", bufs=CONVS))

        w_raws, x_raws, x_groupeds, x_operands, y_banks = {}, {}, {}, {}, {}
        w_sorteds, w_groupeds, w_operands, x1_groupeds, x1_operands = {}, {}, {}, {}, {}

        def live(unit):
            return 0 <= unit < UNITS

        def load_operators(g):
            if g >= GRAPHS:
                return
            w_raw = raw_pool.tile([P, TILES, NODES * OPERATORS], BF16)
            nc.sync.dma_start(out=w_raw[:], in_=W[g].rearrange("(i p) n j -> p i (n j)", p=P))
            w_raws[g] = w_raw

        def load_features(g):
            if g >= GRAPHS:
                return
            x_raw = raw_pool.tile([P, TILES, NODES], BF16)
            nc.sync.dma_start(out=x_raw[:], in_=X[g].rearrange("(i p) n -> p i n", p=P))
            x_raws[g] = x_raw

        load_operators(0)
        load_features(0)
        cv_raws = []
        for cv_w in (cv2_w, cv1_w):
            cv_raw = const.tile([P, CHANNELS], BF16, name="cv_raw%d" % len(cv_raws))
            nc.sync.dma_start(out=cv_raw[:], in_=cv_w)
            cv_raws.append(cv_raw)
        load_operators(1)
        load_features(1)

        mask_all = const.tile([P, GRAPHS, NODES], BF16)
        nc.sync.dma_start(
            out=mask_all[:].rearrange("p g m -> p (g m)"),
            in_=mask.rearrange("g o m -> (g o m)").partition_broadcast(P),
        )

        ident_f32 = const.tile([P, P], F32)
        make_identity(nc, ident_f32[:])
        ident_bf16 = const.tile([P, P], BF16)
        make_identity(nc, ident_bf16[:])
        ones_f32 = const.tile([P, P], F32)
        nc.vector.memset(ones_f32[:], 1.0)
        eps = const.tile([P, 1], F32)
        nc.vector.memset(eps[:], EPS)

        warm = const.tile([P, 1], F32)
        nc.scalar.activation(out=warm[:], in_=eps[:], func=ACT.Sqrt)

        vector_rows = const.tile([P, P], BF16)
        nc.vector.memset(vector_rows[:], 0.0)
        nc.scalar.dma_start(out=vector_rows[0:1, :], in_=cv2_b.unsqueeze(0))
        nc.scalar.dma_start(out=vector_rows[1:2, :], in_=cv1_b.unsqueeze(0))
        nc.scalar.dma_start(out=vector_rows[2:4, :], in_=bn_gamma.rearrange("(h c) -> h c", h=CONVS))
        nc.scalar.dma_start(out=vector_rows[4:6, :], in_=bn_beta.rearrange("(h c) -> h c", h=CONVS))
        per_channel = const.tile([P, 3 * CONVS], F32)
        bias = per_channel[:, 0:CONVS]
        gamma = per_channel[:, CONVS : 2 * CONVS]
        beta = per_channel[:, 2 * CONVS : 3 * CONVS]

        mask_part = const.tile([P, GRAPHS * NODES // P], BF16)
        nc.scalar.dma_start(
            out=mask_part[:], in_=mask.rearrange("g o (q r) -> (g o q) r", r=GRAPHS * NODES // P)
        )
        counts_row = const.tile([P, GRAPHS], BF16)
        nc.vector.memset(counts_row[:], 0.0)
        nc.scalar.dma_start(out=counts_row[0:1, :], in_=N_batch.unsqueeze(0))

        pivot = const.tile([P, CONVS], F32)
        inv_total = const.tile([P, 1], F32)
        ratio_less_2 = const.tile([P, 1], F32)
        offset_0 = const.tile([P, CONVS], F32)
        twice_offset_0 = const.tile([P, CONVS], F32)

        def prepare_channel_vectors():
            vector_cols = tr_psum.tile([P, P], BF16, tag="tr")
            nc.tensor.transpose(vector_cols[:], vector_rows[:], ident_bf16[:])
            nc.vector.tensor_copy(out=per_channel[:], in_=vector_cols[:, 0 : 3 * CONVS])
            nc.vector.tensor_scalar_max(out=pivot[:], in0=bias, scalar1=0.0)

            partial = const.tile([P, 2], F32)
            nc.vector.reduce_sum(out=partial[:, 0:1], in_=mask_part[:], axis=AXIS_X)
            nc.vector.reduce_sum(out=partial[:, 1:2], in_=counts_row[:], axis=AXIS_X)
            totals_psum = tr_psum.tile([P, 2], F32, tag="tr")
            nc.tensor.matmul(out=totals_psum[:], lhsT=ones_f32[:], rhs=partial[:], start=True, stop=True)
            totals = const.tile([P, 2], F32)
            nc.vector.tensor_copy(out=totals[:], in_=totals_psum[:])

            nc.vector.reciprocal(out=inv_total[:], in_=totals[:, 1:2])
            ratio_less_1 = const.tile([P, 1], F32)
            nc.vector.tensor_scalar(
                out=ratio_less_1[:],
                in0=totals[:, 0:1],
                scalar1=inv_total[:],
                scalar2=-1.0,
                op0=ALU.mult,
                op1=ALU.add,
            )
            nc.vector.tensor_scalar_add(out=ratio_less_2[:], in0=ratio_less_1[:], scalar1=-1.0)
            nc.vector.tensor_scalar_mul(out=offset_0[:], in0=pivot[:], scalar1=ratio_less_1[:])
            nc.vector.tensor_scalar_mul(out=twice_offset_0[:], in0=offset_0[:], scalar1=2.0)

        z = const.tile([P, CONVS, GRAPHS, NODES], F32)
        first_parts = const.tile([P, CONVS, GRAPHS], F32)
        second_parts = const.tile([P, CONVS, GRAPHS], F32)

        cv_grouped = const.tile([P, CONVS, OPERATORS, P, PACK], BF16, align_bytes=64)
        cv_codes = const.tile([P, CONVS, OPERATORS, P], U32, align_bytes=64)
        cv_scales = const.tile([P, CONVS, OPERATORS, P], U8, align_bytes=64)

        def transpose_conv_weights():
            for conv in range(CONVS):
                for j in range(OPERATORS):
                    cv_t = tr_psum.tile([P, PACK, P], BF16, tag="tr")
                    for t in range(PACK):
                        first_channel = FEATURES * j + P * t
                        nc.tensor.transpose(
                            cv_t[:, t, :], cv_raws[conv][:, first_channel : first_channel + P], ident_bf16[:]
                        )
                    nc.scalar.copy(out=cv_grouped[:, conv, j], in_=cv_t[:].rearrange("p t o -> p o t"))

        def quantise_conv_weights():
            for conv in range(CONVS):
                for j in range(OPERATORS):
                    nc.vector.quantize_mx(
                        out=cv_codes[:, conv, j, :].bitcast(FP8X4),
                        scales=cv_scales[:, conv, j, :],
                        in_=cv_grouped[:, conv, j].rearrange("p o t -> p (o t)"),
                    )

        def transpose_words(bank, rows_of):
            for u in range(2):
                for i in range(2):
                    nc.tensor.transpose(
                        bank[:, u, P * i : P * (i + 1)],
                        rows_of(i).bitcast(F32)[:, P * u : P * (u + 1)],
                        ident_f32[:],
                    )

        def sort_operator(unit):
            if not live(unit):
                return
            g, j = divmod(unit, OPERATORS)
            w_sorted = unit_pool.tile([P, TILES, NODES], BF16)
            nc.vector.tensor_copy(
                out=w_sorted[:], in_=w_raws[g][:].rearrange("p i (n j) -> p i n j", j=OPERATORS)[:, :, :, j]
            )
            w_sorteds[unit] = w_sorted
            if j == OPERATORS - 1:
                load_operators(g + 2)

        def transpose_features(unit):
            g, j = divmod(unit, OPERATORS)
            if not live(unit) or j != 0:
                return
            x_grouped = graph_pool.tile([P, FEATURES, PACK], BF16, align_bytes=64)
            x_groupeds[g] = x_grouped
            for pair in range(PAIRS):
                x_t = tr_psum.tile([P, 2, PAIR_COLS], F32, tag="tr")
                transpose_words(x_t, lambda i: x_raws[g][:, 2 * pair + i, :])
                copy = nc.vector.tensor_copy if pair == 0 else nc.scalar.copy
                copy(
                    out=x_grouped[:].bitcast(F32)[:, PAIR_COLS * pair : PAIR_COLS * (pair + 1), :],
                    in_=x_t[:].rearrange("p u c -> p c u"),
                )
            load_features(g + 2)

        def transpose_operator(unit):
            if not live(unit):
                return
            w_grouped = unit_pool.tile([P, NODES, PACK], BF16, align_bytes=64)
            w_groupeds[unit] = w_grouped
            for pair in range(PAIRS):
                w_t = tr_psum.tile([P, 2, PAIR_COLS], F32, tag="tr")
                transpose_words(w_t, lambda i: w_sorteds[unit][:, 2 * pair + i, :])
                nc.scalar.copy(
                    out=w_grouped[:].bitcast(F32)[:, PAIR_COLS * pair : PAIR_COLS * (pair + 1), :],
                    in_=w_t[:].rearrange("p u c -> p c u"),
                )

        def quantise(grouped, pool, kind):
            codes = pool.tile([P, NODES], U32, align_bytes=64, name=kind + "_codes")
            scales = pool.tile([P, NODES], U8, align_bytes=64, name=kind + "_scales")
            nc.vector.quantize_mx(
                out=codes[:].bitcast(FP8X4), scales=scales[:], in_=grouped[:].rearrange("p c t -> p (c t)")
            )
            return codes, scales

        def quantise_operator(unit):
            if not live(unit):
                return
            g, j = divmod(unit, OPERATORS)
            w_operands[unit] = quantise(w_groupeds[unit], unit_pool, "w")
            if j == 0:
                x_operands[g] = quantise(x_groupeds[g], graph_pool, "x")

        def apply_operator(unit):
            if not live(unit):
                return
            x_codes, x_scales = x_operands[unit // OPERATORS]
            w_codes, w_scales = w_operands[unit]
            x1_grouped = unit_pool.tile([P, NODES, PACK], BF16, align_bytes=64)
            x1_groupeds[unit] = x1_grouped
            for i in range(TILES):
                m_cols = slice(P * i, P * (i + 1))
                x1_bank = x1_psum.tile([P, PACK, P], F32)
                for t in range(PACK):
                    f_cols = slice(P * t, P * (t + 1))
                    nc.tensor.matmul_mx(
                        out=x1_bank[:, t, :],
                        lhsT=x_codes[:, f_cols].bitcast(FP8X4),
                        lhsT_scale=x_scales[:, f_cols],
                        rhs=w_codes[:, m_cols].bitcast(FP8X4),
                        rhs_scale=w_scales[:, m_cols],
                        start=True,
                        stop=True,
                    )
                nc.scalar.copy(out=x1_grouped[:, m_cols, :], in_=x1_bank[:].rearrange("p t m -> p m t"))

        def quantise_x1(unit):
            if live(unit):
                x1_operands[unit] = quantise(x1_groupeds[unit], unit_pool, "x1")

        def convolve(unit):
            if not live(unit):
                return
            g, j = divmod(unit, OPERATORS)
            x1_codes, x1_scales = x1_operands[unit]
            for conv in range(CONVS):
                if j == 0:
                    y = y_psum.tile([P, NODES], F32)
                    y_banks[g, conv] = y
                nc.tensor.matmul_mx(
                    out=y_banks[g, conv][:],
                    lhsT=cv_codes[:, conv, j, :].bitcast(FP8X4),
                    lhsT_scale=cv_scales[:, conv, j, :],
                    rhs=x1_codes[:].bitcast(FP8X4),
                    rhs_scale=x1_scales[:],
                    start=(j == 0),
                    stop=(j == OPERATORS - 1),
                )
            if j == OPERATORS - 1:
                for conv in range(CONVS):
                    nc.scalar.activation(
                        out=z[:, conv, g, :],
                        in_=y_banks[g, conv][:],
                        func=ACT.Relu,
                        bias=bias[:, conv : conv + 1],
                    )

        def add_to_statistics(unit):
            g, j = divmod(unit, OPERATORS)
            if not live(unit) or j != OPERATORS - 1:
                return
            weighted = []
            for conv in range(CONVS):
                masked = stat_pool.tile([P, NODES], F32)
                nc.vector.scalar_tensor_tensor(
                    out=masked[:],
                    in0=z[:, conv, g, :],
                    scalar=pivot[:, conv : conv + 1],
                    in1=mask_all[:, g, :],
                    op0=ALU.subtract,
                    op1=ALU.mult,
                    accum_out=first_parts[:, conv, g : g + 1],
                )
                weighted.append(masked)
            for conv in range(CONVS):
                squares = stat_pool.tile([P, NODES], F32)
                nc.vector.scalar_tensor_tensor(
                    out=squares[:],
                    in0=z[:, conv, g, :],
                    scalar=pivot[:, conv : conv + 1],
                    in1=weighted[conv][:],
                    op0=ALU.subtract,
                    op1=ALU.mult,
                    accum_out=second_parts[:, conv, g : g + 1],
                )

        for turn in range(-SORT_AHEAD, UNITS + STATISTICS_LAG + 1):
            transpose_features(turn)
            transpose_operator(turn)
            if turn == 0:
                transpose_conv_weights()
            apply_operator(turn - STEP_1_LAG)
            convolve(turn - STEP_2_LAG)
            quantise_x1(turn - QUANTISE_X1_LAG)
            quantise_operator(turn - QUANTISE_W_LAG)
            if turn == 1:
                quantise_conv_weights()
                prepare_channel_vectors()
            add_to_statistics(turn - STATISTICS_LAG)
            sort_operator(turn + SORT_AHEAD)

        first = const.tile([P, CONVS], F32)
        nc.vector.reduce_sum(out=first[:], in_=first_parts[:], axis=AXIS_X)
        second = const.tile([P, CONVS], F32)
        nc.vector.reduce_sum(out=second[:], in_=second_parts[:], axis=AXIS_X)
        offset = const.tile([P, CONVS], F32)
        nc.vector.scalar_tensor_tensor(
            out=offset[:], in0=first[:], scalar=inv_total[:], in1=offset_0[:], op0=ALU.mult, op1=ALU.add
        )
        inner = const.tile([P, CONVS], F32)
        nc.vector.scalar_tensor_tensor(
            out=inner[:], in0=offset[:], scalar=ratio_less_2[:], in1=twice_offset_0[:], op0=ALU.mult, op1=ALU.add
        )
        correction = const.tile([P, CONVS], F32)
        nc.vector.tensor_mul(out=correction[:], in0=inner[:], in1=offset[:])
        var = const.tile([P, CONVS], F32)
        nc.vector.scalar_tensor_tensor(
            out=var[:], in0=second[:], scalar=inv_total[:], in1=correction[:], op0=ALU.mult, op1=ALU.add
        )
        std = const.tile([P, CONVS], F32)
        nc.scalar.activation(out=std[:], in_=var[:], func=ACT.Sqrt, bias=eps[:])
        mean = const.tile([P, CONVS], F32)
        nc.vector.tensor_add(out=mean[:], in0=offset[:], in1=pivot[:])
        inv_std = const.tile([P, CONVS], F32)
        nc.vector.reciprocal(out=inv_std[:], in_=std[:])
        gain = const.tile([P, CONVS], F32)
        nc.vector.tensor_mul(out=gain[:], in0=gamma, in1=inv_std[:])
        mean_gain = const.tile([P, CONVS], F32)
        nc.vector.tensor_mul(out=mean_gain[:], in0=mean[:], in1=gain[:])
        shift = const.tile([P, CONVS], F32)
        nc.vector.tensor_sub(out=shift[:], in0=beta, in1=mean_gain[:])

        for g in range(GRAPHS):
            for conv in range(CONVS):
                piece = z[:, conv, g, :]
                nc.scalar.activation(
                    out=piece,
                    in_=piece,
                    func=ACT.Identity,
                    scale=gain[:, conv : conv + 1],
                    bias=shift[:, conv : conv + 1],
                )
                nc.vector.tensor_mul(out=piece, in0=piece, in1=mask_all[:, g, :])
                nc.sync.dma_start(out=out[g, P * conv : P * (conv + 1), :], in_=piece)
